import numpy as np
import ml_dtypes


def mxq(x, axis, fmt="e4m3"):
    dtype, down = {"e4m3": (ml_dtypes.float8_e4m3fn, 7), "e5m2": (ml_dtypes.float8_e5m2, 14)}[fmt]
    v = np.moveaxis(np.asarray(x, np.float32).astype(ml_dtypes.bfloat16).astype(np.float64), axis, -1)
    blocks = v.reshape(v.shape[:-1] + (-1, 32))
    amax = np.abs(blocks).max(-1, keepdims=True)
    byte = np.maximum(np.where(amax > 0, np.frexp(amax)[1] - 1 + 127, 0) - down, 1)
    scale = np.exp2(byte - 127.0)
    codes = (blocks / scale).astype(np.float32).astype(dtype).astype(np.float64)
    return np.moveaxis((codes * scale).reshape(v.shape), -1, axis)


WIDE = False


def mx_kscale(k):
    if not WIDE:
        return np.ones(k)
    levels = np.array([10, -10, 5, -5, 0])
    if k % 512:
        return np.exp2(np.random.permutation(np.resize(levels, k // 32))).repeat(32)
    a = np.empty((k // 512, 16))
    for p in range(k // 512):
        a[p, :8] = np.random.permutation(np.resize(levels, 8))
        for g in range(8):
            far = levels[np.abs(levels - a[p, g]) >= 10]
            a[p, g + 8] = far[np.random.randint(len(far))]
    return np.exp2(a.ravel()).repeat(32)


BF16 = ml_dtypes.bfloat16


def bf(x):
    return np.asarray(x, np.float32).astype(BF16)


def f64(x):
    return np.asarray(x).astype(np.float64)


B, E, D1, D2, WS1, WS2, H, HID = 2, 1024, 32, 16, 8, 8, 32, 2048
NW = (D1 // WS1) * (D2 // WS2)
S = WS1 * WS2
DH = E // H


def draw0():
    n = np.random.standard_normal
    s = mx_kscale(E)
    return {"z_heads": bf(n((B, NW, H, S, DH)) * 0.4 * s.reshape(H, 1, DH)),
            "x": bf(n((B, E, D1, D2))),
            "Wo": bf(n((E, E)) / np.sqrt(E) / s[:, None]),
            "bo": bf(0.1 * n(E))}


def core(z_heads, x, Wo, bo):
    z = f64(z_heads).transpose(0, 1, 3, 2, 4).reshape(B, NW, S, E)
    z = (mxq(z, 3, "e4m3") @ mxq(f64(Wo), 0, "e4m3")) + f64(bo)
    z = z.reshape(B, D1 // WS1, D2 // WS2, WS1, WS2, E).transpose(0, 1, 3, 2, 4, 5).reshape(B, D1, D2, E)
    z = np.roll(z, (WS1 // 2, WS2 // 2), axis=(1, 2))
    return f64(x).transpose(0, 2, 3, 1) + z


def e4m3fn_bytes(y):
    return np.clip(np.asarray(y, np.float64), -448.0, 448.0).astype(np.float32).astype(ml_dtypes.float8_e4m3fn).view(np.uint8)


def e4m3fn_values(b):
    return np.asarray(b, np.uint8).view(ml_dtypes.float8_e4m3fn).astype(np.float64)


def setup_inputs():
    d = draw0()
    x0 = np.asarray(d['z_heads']).astype(np.float64)
    s = (np.max(np.abs(x0), axis=(0, 1, 3, 4), keepdims=True) / 448.0).astype(np.float32)
    out = {}
    for k, v in d.items():
        if k == 'z_heads':
            out['z_heads_bytes'] = e4m3fn_bytes(x0 / s.astype(np.float64))
            out['z_heads_scale'] = s
        else:
            out[k] = v
    return out


def reference(z_heads_bytes, z_heads_scale, x, Wo, bo):
    return core(e4m3fn_values(z_heads_bytes) * z_heads_scale.astype(np.float64), x, Wo, bo)

@@ -1,0 +1,233 @@
+from contextlib import ExitStack
+
+import concourse.mybir as mybir
+from concourse.masks import make_identity
+
+F32 = mybir.dt.float32
+BF16 = mybir.dt.bfloat16
+U8 = mybir.dt.uint8
+U32 = mybir.dt.uint32
+FP8 = mybir.dt.float8_e4m3fn
+FP8X4 = mybir.dt.float8_e4m3fn_x4
+ALU = mybir.AluOpType
+ACT = mybir.ActivationFunctionType
+
+FLOPS = 2 * 1024 * 1024 * 1024
+
+P = 128
+VW = [1280,1280]
+LOADS = ["z10","z11","z01","z00","W10","W00","W11","W01","x01","x11","x10","x00"]
+ON_VECTOR = ["E1_11","Iw10","Iw00","Iw11","E2_11","E2_00"]
+STEPS = ["wdS10","wdV10","wdV11","wdS11","wdV01","wdS01","T1_13","T1_11","wdV00","B0","wdS00","T1_10","E1_11","T1_12","E1_10","Iw10","T1_02","E1_12","T1_00","E1_13","T1_01","Iw00","E1_00","B1","T2_10","E1_01","T1_03","E1_02","B2","Qw10","T2_111","T2_113","E1_03","T2_112","Iw11","T2_110","E2_13","T2_00","E2_12","E2_11","T2_011","E2_10","T2_013","T2_012","Qw00","T2_010","E2_02","Qz10","E2_03","Qz11","E2_01","E2_00","Iw01","MX11","Qw11","MX01","Qz00","MX21","Qz01","MX31","ST11","MX20","Qw01","MX30","ST31","MX10","ST01","MX40","ST10","MX00","ST20","MX50","ST30","MX60","ST00","MX71","ST21","T3_030","ST60","T3_010","E3_030","T3_100","ST50","T3_110","E3_010","T3_130","ST71","T3_120","E3_110","ST40","MX70","E3_120","MX51","E3_130","ST70","T3_000","E3_100","T3_021","E3_000","T3_031","T3_011","E3_031","MX61","E3_021","MX41","ST61","E3_011","T3_001","ST51","T3_020","E3_001","ST41","E3_020","T3_121","T3_131","E3_121","T3_111","T3_101","E3_131","E3_111","E3_101"]
+MANUAL = True
+WARM_T = 0
+
+
+def tile_functatransformer_pb_kernel(tc, z_heads_bytes, z_heads_scale, x, Wo, bo, out):
+    nc = tc.nc
+    with ExitStack() as ctx:
+        keep = ctx.enter_context(tc.tile_pool(name="keep", bufs=1))
+        psum = ctx.enter_context(tc.psum_pool(name="psum", bufs=8))
+        if MANUAL:
+            ctx.enter_context(tc.manual_schedule())
+
+        sc = keep.tile([P, 1], F32, name="sc")
+        scale_rows = z_heads_scale.rearrange("a b h c d -> h (a b c d)")
+        for sh in range(4):
+            nc.scalar.dma_start(out=sc[sh:P:4, :], in_=scale_rows)
+        bz = keep.tile([P, P], BF16, name="bz")
+        nc.gpsimd.memset(bz[:], 0.0)
+        nc.scalar.dma_start(out=bz[0:8, :], in_=bo.rearrange("(et p) -> et p", p=P))
+
+        zb = {}
+        wraw = {}
+        xs = {}
+        wo_v = Wo.rearrange("(g p t) n -> g p t n", g=2, p=P, t=4)
+        for name in LOADS:
+            i = int(name[1])
+            if name.startswith("z"):
+                h = int(name[2])
+                t = keep.tile([P, 4, 512], U8, name="zbytes%d%d" % (i, h))
+                src = z_heads_bytes[i].rearrange("w h (sh sl) d -> (h sh) w (sl d)", sh=4)
+                nc.sync.dma_start(out=t[:], in_=src[:, 4 * h:4 * h + 4, :])
+                zb[(i, h)] = t
+            elif name.startswith("W"):
+                eh = int(name[2])
+                t = keep.tile([P, 4, 512], BF16, name="wraw%d%d" % (i, eh))
+                nc.sync.dma_start(out=t[:], in_=wo_v[i][:, :, 512 * eh:512 * (eh + 1)])
+                wraw[(i, eh)] = t
+            else:
+                eh = int(name[2])
+                t = keep.tile([P, 4, 512], BF16, name="xs%d%d" % (i, eh))
+                src = x[i].rearrange("(et p) i j -> p et (i j)", p=P)
+                nc.sync.dma_start(out=t[:], in_=src[:, 4 * eh:4 * eh + 4, :])
+                xs[(i, eh)] = t
+
+        warm = keep.tile([P, 2], F32, name="warm")
+        nc.vector.memset(warm[:], 0.0)
+        nc.scalar.activation(out=warm[:, 1:2], in_=warm[:, 0:1], func=ACT.Copy)
+
+        ident = keep.tile([P, P], F32, name="ident")
+        make_identity(nc, ident[:])
+        p1 = keep.tile([P, P], F32, name="p1")
+        nc.vector.tensor_copy(
+            out=p1[:].rearrange("p (g s h) -> p g s h", g=2, s=4),
+            in_=ident[:].rearrange("p (g h s) -> p g s h", g=2, s=4),
+        )
+        pa = keep.tile([P, P], F32, name="pa")
+        pa_v = pa[:].rearrange("p (w s j) -> p w s j", w=4, s=2)
+        id_v = ident[:].rearrange("p (w v s k) -> p w v s k", w=4, v=2, s=2)
+        nc.vector.tensor_copy(out=pa_v[:, :, :, 4:12], in_=id_v[:, :, 0, :, 0:8])
+        nc.vector.tensor_copy(out=pa_v[:, :, :, 12:16], in_=id_v[:, :, 1, :, 0:4])
+        nc.vector.tensor_copy(out=pa_v[:, :, :, 0:4], in_=id_v[:, :, 1, :, 4:8])
+        pb = keep.tile([P, P], F32, name="pb")
+        nc.vector.tensor_copy(out=pb[:, 32:128], in_=pa[:, 0:96])
+        nc.vector.tensor_copy(out=pb[:, 0:32], in_=pa[:, 96:128])
+        bzf = keep.tile([P, P], F32, name="bzf")
+        bo_col = keep.tile([P, 8], F32, name="bo_col")
+
+        if WARM_T > 0:
+            wps = psum.tile([P, 4, P], F32, name="wps", tag="bank")
+            for i in range(WARM_T):
+                nc.tensor.transpose(out=wps[:, i % 4, :], in_=ident[:], identity=ident[:])
+
+        a = {}
+        c = {}
+        gq = {}
+        for b in range(2):
+            a[b] = keep.tile([P, 4096], BF16, name="a%d" % b)
+            c[b] = keep.tile([P, 2, P, 8], F32, name="c%d" % b)
+            gq[b] = keep.tile([P, 4096], BF16, name="gq%d" % b, align_bytes=64)
+        bank = {}
+        zc = {}
+        zs = {}
+        wgrp = {}
+        wc = {}
+        ws = {}
+        res = {}
+        out_v = out.rearrange("b i j e -> b (i j) e")
+
+        def copy_on(name, o, i):
+            if name in ON_VECTOR:
+                nc.vector.tensor_copy(out=o, in_=i)
+            else:
+                nc.scalar.copy(out=o, in_=i)
+
+        for s in STEPS:
+            if s.startswith("wd"):
+                b = int(s[3])
+                h = int(s[4])
+                zf = zb[(b, h)][:].rearrange("p w c -> p (w c)").bitcast(FP8)
+                dst = a[b][:, 2048 * h:2048 * (h + 1)]
+                v = VW[b]
+                if s[2] == "V":
+                    nc.vector.tensor_scalar(out=dst[:, 0:v], in0=zf[:, 0:v], scalar1=sc[:, 0:1], scalar2=None, op0=ALU.mult)
+                else:
+                    nc.scalar.activation(out=dst[:, v:2048], in_=zf[:, v:2048], func=ACT.Copy, scale=sc[:, 0:1])
+            elif s.startswith("T1_"):
+                b = int(s[3])
+                k = int(s[4])
+                t1 = psum.tile([P, 4, P], F32, name="t1", tag="bank")
+                aw = a[b][:].bitcast(F32)
+                for j in range(4):
+                    dp = 2 * (4 * (k % 2) + j) + k // 2
+                    nc.tensor.transpose(out=t1[:, j, :], in_=aw[:, dp:2048:16], identity=p1[:])
+                bank[s] = t1
+            elif s.startswith("E1_"):
+                b = int(s[3])
+                k = int(s[4])
+                dq0 = 4 * (k % 2)
+                copy_on(s, c[b][:, k // 2, :, dq0:dq0 + 4], bank["T1_" + s[3:]][:].rearrange("p s x -> p x s"))
+            elif s.startswith("T2_"):
+                b = int(s[3])
+                u = int(s[4])
+                cw = c[b][:].rearrange("p u x q -> p u (x q)")
+                if u == 0:
+                    shs = [0, 1, 2, 3]
+                    for sh in shs:
+                        t2 = psum.tile([P, 2, 2, P], F32, name="t2", tag="bank")
+                        bank["T2_%d%d" % (b, sh)] = t2
+                else:
+                    shs = [int(s[5])]
+                for sh in shs:
+                    perm = pa if sh < 2 else pb
+                    for g in range(2):
+                        y = 4 * g + sh
+                        nc.tensor.transpose(out=bank["T2_%d%d" % (b, sh)][:, u, g, :], in_=cw[:, u, y * P:(y + 1) * P], identity=perm[:])
+            elif s.startswith("E2_"):
+                b = int(s[3])
+                sh = int(s[4])
+                r0 = 32 * ((2 * sh + 4) % 8)
+                gw = gq[b][:].bitcast(F32).rearrange("p (y r) -> p y r", y=8)
+                copy_on(
+                    s,
+                    gw[:, :, r0:r0 + 64].rearrange("p y (x u) -> p y x u", u=2),
+                    bank["T2_%d%d" % (b, sh)][:].rearrange("p u g (w x) -> p (g w) x u", w=4),
+                )
+            elif s.startswith("Qz"):
+                b = int(s[2])
+                g = int(s[3])
+                zc[(b, g)] = keep.tile([P, 512], U32, name="zc%d%d" % (b, g), align_bytes=64)
+                zs[(b, g)] = keep.tile([P, 512], U8, name="zs%d%d" % (b, g), align_bytes=64)
+                nc.vector.quantize_mx(out=zc[(b, g)][:].bitcast(FP8X4), scales=zs[(b, g)][:], in_=gq[b][:, 2048 * g:2048 * (g + 1)])
+            elif s.startswith("Iw"):
+                g = int(s[2])
+                eh = int(s[3])
+                wgrp[(g, eh)] = keep.tile([P, 512, 4], BF16, name="wgrp%d%d" % (g, eh), align_bytes=64)
+                copy_on(s, wgrp[(g, eh)][:], wraw[(g, eh)][:].rearrange("p t n -> p n t"))
+            elif s.startswith("Qw"):
+                g = int(s[2])
+                eh = int(s[3])
+                wc[(g, eh)] = keep.tile([P, 512], U32, name="wc%d%d" % (g, eh), align_bytes=64)
+                ws[(g, eh)] = keep.tile([P, 512], U8, name="ws%d%d" % (g, eh), align_bytes=64)
+                nc.vector.quantize_mx(out=wc[(g, eh)][:].bitcast(FP8X4), scales=ws[(g, eh)][:], in_=wgrp[(g, eh)][:].rearrange("p n t -> p (n t)"))
+            elif s.startswith("MX"):
+                et = int(s[2])
+                b = int(s[3])
+                eh = et // 4
+                el = et % 4
+                acc = psum.tile([P, 512], F32, name="acc", tag="bank")
+                for g in range(2):
+                    nc.tensor.matmul_mx(
+                        out=acc[:],
+                        lhsT=wc[(g, eh)][:, P * el:P * (el + 1)].bitcast(FP8X4),
+                        lhsT_scale=ws[(g, eh)][:, P * el:P * (el + 1)],
+                        rhs=zc[(b, g)][:].bitcast(FP8X4),
+                        rhs_scale=zs[(b, g)][:],
+                        start=(g == 0),
+                        stop=(g == 1),
+                    )
+                bank[s] = acc
+            elif s.startswith("ST"):
+                et = int(s[2])
+                b = int(s[3])
+                res[(et, b)] = keep.tile([P, 512], F32, name="res%d%d" % (et, b))
+                nc.vector.scalar_tensor_tensor(
+                    out=res[(et, b)][:], in0=bank["MX" + s[2:]][:], scalar=bo_col[:, et:et + 1],
+                    in1=xs[(b, et // 4)][:, et % 4, :], op0=ALU.add, op1=ALU.add,
+                )
+            elif s.startswith("T3_"):
+                b = int(s[3])
+                pt = int(s[4])
+                eh = int(s[5])
+                t3 = psum.tile([P, 4, P], F32, name="t3", tag="bank")
+                for el in range(4):
+                    nc.tensor.transpose(out=t3[:, el, :], in_=res[(4 * eh + el, b)][:, P * pt:P * (pt + 1)], identity=ident[:])
+                bank[s] = t3
+            elif s.startswith("E3_"):
+                b = int(s[3])
+                pt = int(s[4])
+                eh = int(s[5])
+                o = keep.tile([P, 512], F32, name="o" + s[3:])
+                copy_on(s, o[:], bank["T3_" + s[3:]][:].rearrange("p s x -> p (s x)"))
+                nc.sync.dma_start(out=out_v[b, P * pt:P * (pt + 1), 512 * eh:512 * (eh + 1)], in_=o[:])
+            elif s == "B0":
+                nc.vector.tensor_copy(out=bzf[:], in_=bz[:])
+            elif s == "B1":
+                bo_ps = psum.tile([P, 512], F32, name="bo_ps", tag="bank")
+                nc.tensor.transpose(out=bo_ps[:, 0:P], in_=bzf[:], identity=ident[:])
+                bank[s] = bo_ps
+            elif s == "B2":
+                nc.vector.tensor_copy(out=bo_col[:], in_=bank["B1"][:, 0:8])
+            else:
+                assert False, s

@@ -18,9 +18,10 @@ P = 128
 VW = [1280,1280]
 LOADS = ["z10","z11","z01","z00","W10","W00","W11","W01","x01","x11","x10","x00"]
 ON_VECTOR = ["E1_11","Iw10","Iw00","Iw11","E2_11","E2_00"]
-STEPS = ["wdS10","wdV10","wdV11","wdS11","wdV01","wdS01","T1_13","T1_11","wdV00","B0","wdS00","T1_10","E1_11","T1_12","E1_10","Iw10","T1_02","E1_12","T1_00","E1_13","T1_01","Iw00","E1_00","B1","T2_10","E1_01","T1_03","E1_02","B2","Qw10","T2_111","T2_113","E1_03","T2_112","Iw11","T2_110","E2_13","T2_00","E2_12","E2_11","T2_011","E2_10","T2_013","T2_012","Qw00","T2_010","E2_02","Qz10","E2_03","Qz11","E2_01","E2_00","Iw01","MX11","Qw11","MX01","Qz00","MX21","Qz01","MX31","ST11","MX20","Qw01","MX30","ST31","MX10","ST01","MX40","ST10","MX00","ST20","MX50","ST30","MX60","ST00","MX71","ST21","T3_030","ST60","T3_010","E3_030","T3_100","ST50","T3_110","E3_010","T3_130","ST71","T3_120","E3_110","ST40","MX70","E3_120","MX51","E3_130","ST70","T3_000","E3_100","T3_021","E3_000","T3_031","T3_011","E3_031","MX61","E3_021","MX41","ST61","E3_011","T3_001","ST51","T3_020","E3_001","ST41","E3_020","T3_121","T3_131","E3_121","T3_111","T3_101","E3_131","E3_111","E3_101"]
+STEPS = ["wdS10","wdV10","wdV11","wdS11","wdV01","wdS01","T1_13","T1_11","wdV00","B0","wdS00","T1_10","E1_11","T1_12","E1_10","Iw10","T1_02","E1_12","T1_00","E1_13","T1_01","Iw00","E1_00","B1","T2_10","E1_01","T1_03","E1_02","B2","Qw10","T2_111","T2_113","E1_03","T2_112","Iw11","T2_110","E2_13","T2_00","E2_12","E2_11","T2_011","E2_10","T2_013","T2_012","Qw00","T2_010","D","D","D","D","E2_02","Qz10","E2_03","Qz11","E2_01","E2_00","Iw01","MX11","Qw11","MX01","Qz00","MX21","Qz01","MX31","ST11","MX20","Qw01","MX30","ST31","MX10","ST01","MX40","ST10","MX00","ST20","MX50","ST30","MX60","ST00","MX71","ST21","T3_030","ST60","T3_010","E3_030","T3_100","ST50","T3_110","E3_010","T3_130","ST71","T3_120","E3_110","ST40","MX70","E3_120","MX51","E3_130","ST70","T3_000","E3_100","T3_021","E3_000","T3_031","T3_011","E3_031","MX61","E3_021","MX41","ST61","E3_011","T3_001","ST51","T3_020","E3_001","ST41","E3_020","T3_121","T3_131","E3_121","T3_111","T3_101","E3_131","E3_111","E3_101"]
 MANUAL = True
 WARM_T = 0
+WARM_MM = 8
 
 
 def tile_functatransformer_pb_kernel(tc, z_heads_bytes, z_heads_scale, x, Wo, bo, out):
@@ -31,6 +32,12 @@ def tile_functatransformer_pb_kernel(tc, z_heads_bytes, z_heads_scale, x, Wo, bo
         if MANUAL:
             ctx.enter_context(tc.manual_schedule())
 
+        wz = keep.tile([P, 512], BF16, name="wz")
+        nc.vector.memset(wz[:], 0.0)
+        if WARM_MM > 0:
+            wmm = psum.tile([P, 512], F32, name="wmm", tag="bank")
+            for i in range(WARM_MM):
+                nc.tensor.matmul(out=wmm[:], lhsT=wz[:, 0:P], rhs=wz[:], start=True, stop=True)
         sc = keep.tile([P, 1], F32, name="sc")
         scale_rows = z_heads_scale.rearrange("a b h c d -> h (a b c d)")
         for sh in range(4):
@@ -221,6 +228,8 @@ def tile_functatransformer_pb_kernel(tc, z_heads_bytes, z_heads_scale, x, Wo, bo
                 o = keep.tile([P, 512], F32, name="o" + s[3:])
                 copy_on(s, o[:], bank["T3_" + s[3:]][:].rearrange("p s x -> p (s x)"))
                 nc.sync.dma_start(out=out_v[b, P * pt:P * (pt + 1), 512 * eh:512 * (eh + 1)], in_=o[:])
+            elif s == "D":
+                nc.tensor.matmul(out=wmm[:], lhsT=wz[:, 0:P], rhs=wz[:], start=True, stop=True)
             elif s == "B0":
                 nc.vector.tensor_copy(out=bzf[:], in_=bz[:])
             elif s == "B1":

@@ -16,12 +16,12 @@ FLOPS = 2 * 1024 * 1024 * 1024
 
 P = 128
 VW = [1280,1280]
-LOADS = ["z10","z11","z01","z00","W10","W00","W11","W01","x01","x11","x10","x00"]
-ON_VECTOR = ["E1_11","Iw10","Iw00","Iw11","E2_11","E2_00"]
-STEPS = ["wdS10","wdV10","wdV11","wdS11","wdV01","wdS01","T1_13","T1_11","wdV00","B0","wdS00","T1_10","E1_11","T1_12","E1_10","Iw10","T1_02","E1_12","T1_00","E1_13","T1_01","Iw00","E1_00","B1","T2_10","E1_01","T1_03","E1_02","B2","Qw10","T2_111","T2_113","E1_03","T2_112","Iw11","T2_110","E2_13","T2_00","E2_12","E2_11","T2_011","E2_10","T2_013","T2_012","Qw00","T2_010","D","D","D","D","E2_02","Qz10","E2_03","Qz11","E2_01","E2_00","Iw01","MX11","Qw11","MX01","Qz00","MX21","Qz01","MX31","ST11","MX20","Qw01","MX30","ST31","MX10","ST01","MX40","ST10","MX00","ST20","MX50","ST30","MX60","ST00","MX71","ST21","T3_030","ST60","T3_010","E3_030","T3_100","ST50","T3_110","E3_010","T3_130","ST71","T3_120","E3_110","ST40","MX70","E3_120","MX51","E3_130","ST70","T3_000","E3_100","T3_021","E3_000","T3_031","T3_011","E3_031","MX61","E3_021","MX41","ST61","E3_011","T3_001","ST51","T3_020","E3_001","ST41","E3_020","T3_121","T3_131","E3_121","T3_111","T3_101","E3_131","E3_111","E3_101"]
+LOADS = ["z00","z01","z10","z11","W00","W10","W01","W11","x00","x01","x10","x11"]
+ON_VECTOR = ["E1_00","E1_01","Iw00","Iw10","E2_00","E1_12","Iw11","E3_020","E3_111","E3_131"]
+STEPS = ["wdS00","wdV00","wdV01","wdS01","wdV10","wdS10","T1_00","T1_01","wdV11","B0","wdS11","T1_02","E1_00","T1_03","E1_01","E1_02","Iw00","E1_03","B1","T2_00","T2_010","T2_011","Iw10","T2_012","T2_013","E2_01","T1_10","T1_11","E2_02","E2_00","T1_12","E2_03","B2","Qw00","T1_13","E1_10","Qw10","E1_11","Qz00","E1_13","T2_10","Qz01","Iw01","E1_12","Iw11","T2_110","T2_111","T2_112","T2_113","MX00","E2_10","MX10","Qw01","E2_11","MX20","Qw11","E2_12","MX30","ST00","E2_13","MX40","ST10","MX50","ST20","MX60","ST30","MX70","Qz10","T3_000","Qz11","T3_010","ST40","E3_000","T3_020","T3_030","ST50","E3_010","MX01","ST60","E3_030","MX11","ST70","MX21","ST01","MX31","ST11","T3_001","E3_020","T3_011","E3_001","T3_021","ST21","T3_031","E3_011","ST31","MX41","E3_021","MX51","E3_031","ST41","MX61","ST51","MX71","ST61","T3_100","ST71","T3_110","E3_100","T3_120","T3_130","E3_110","T3_101","T3_111","E3_120","T3_121","E3_130","E3_111","T3_131","E3_101","E3_131","E3_121"]
 MANUAL = True
 WARM_T = 0
-WARM_MM = 8
+WARM_MM = 0
 
 
 def tile_functatransformer_pb_kernel(tc, z_heads_bytes, z_heads_scale, x, Wo, bo, out):
@@ -181,7 +181,11 @@ def tile_functatransformer_pb_kernel(tc, z_heads_bytes, z_heads_scale, x, Wo, bo
                 g = int(s[2])
                 eh = int(s[3])
                 wgrp[(g, eh)] = keep.tile([P, 512, 4], BF16, name="wgrp%d%d" % (g, eh), align_bytes=64)
-                copy_on(s, wgrp[(g, eh)][:], wraw[(g, eh)][:].rearrange("p t n -> p n t"))
+                copy_on(
+                    s,
+                    wgrp[(g, eh)][:].rearrange("p (c i) t -> p c t i", i=4),
+                    wraw[(g, eh)][:].rearrange("p t (c i) -> p c t i", i=4),
+                )
             elif s.startswith("Qw"):
                 g = int(s[2])
                 eh = int(s[3])

@@ -16,9 +16,10 @@ FLOPS = 2 * 1024 * 1024 * 1024
 
 P = 128
 VW = [1280,1280]
-LOADS = ["z00","z01","z10","z11","W00","W10","W01","W11","x00","x01","x10","x11"]
-ON_VECTOR = ["E1_00","E1_01","Iw00","Iw10","E2_00","E1_12","Iw11","E3_020","E3_111","E3_131"]
-STEPS = ["wdS00","wdV00","wdV01","wdS01","wdV10","wdS10","T1_00","T1_01","wdV11","B0","wdS11","T1_02","E1_00","T1_03","E1_01","E1_02","Iw00","E1_03","B1","T2_00","T2_010","T2_011","Iw10","T2_012","T2_013","E2_01","T1_10","T1_11","E2_02","E2_00","T1_12","E2_03","B2","Qw00","T1_13","E1_10","Qw10","E1_11","Qz00","E1_13","T2_10","Qz01","Iw01","E1_12","Iw11","T2_110","T2_111","T2_112","T2_113","MX00","E2_10","MX10","Qw01","E2_11","MX20","Qw11","E2_12","MX30","ST00","E2_13","MX40","ST10","MX50","ST20","MX60","ST30","MX70","Qz10","T3_000","Qz11","T3_010","ST40","E3_000","T3_020","T3_030","ST50","E3_010","MX01","ST60","E3_030","MX11","ST70","MX21","ST01","MX31","ST11","T3_001","E3_020","T3_011","E3_001","T3_021","ST21","T3_031","E3_011","ST31","MX41","E3_021","MX51","E3_031","ST41","MX61","ST51","MX71","ST61","T3_100","ST71","T3_110","E3_100","T3_120","T3_130","E3_110","T3_101","T3_111","E3_120","T3_121","E3_130","E3_111","T3_131","E3_101","E3_131","E3_121"]
+LOADS = ["z00","z01","z10","z11","W00","W10","x00","x10","W01","W11","x01","x11"]
+ON_VECTOR = ["E1_02","E2_00","E2_01","E1_10","E2_11","E2_12","E3_101"]
+ON_GPSIMD = ["Iw00","Iw10","Iw01","Iw11"]
+STEPS = ["wdS00","wdV00","wdV01","wdS01","wdV10","wdS10","T1_00","T1_01","wdV11","B0","E1_00","T1_02","E1_01","T1_03","E1_02","Iw00","B1","T2_00","E1_03","wdS11","T2_010","T2_011","T2_012","E2_00","T2_013","T1_10","E2_03","E2_01","T1_11","E2_02","Iw10","B2","Qw00","T1_12","E1_10","E1_11","T1_13","E1_12","Qz00","T2_10","E1_13","Qz01","T2_110","T2_111","T2_112","Qw10","Iw01","E2_10","T2_113","E2_11","E2_13","MX00","E2_12","MX10","Qz10","MX20","Qz11","MX30","Iw11","ST00","MX01","ST10","MX11","ST30","MX21","ST20","MX31","Qw01","T3_000","Qw11","T3_010","E3_000","T3_020","ST11","T3_030","ST01","MX40","E3_030","ST21","MX50","E3_020","ST31","MX60","MX70","ST60","T3_100","ST40","T3_110","T3_120","ST50","E3_110","T3_130","ST70","MX41","E3_120","MX51","E3_100","ST41","MX61","E3_010","ST51","MX71","E3_130","T3_001","ST71","T3_011","E3_001","T3_021","ST61","T3_031","E3_021","T3_101","T3_111","E3_011","E3_101","T3_121","T3_131","E3_031","E3_111","E3_131","E3_121"]
 MANUAL = True
 WARM_T = 0
 WARM_MM = 0
@@ -181,11 +182,19 @@ def tile_functatransformer_pb_kernel(tc, z_heads_bytes, z_heads_scale, x, Wo, bo
                 g = int(s[2])
                 eh = int(s[3])
                 wgrp[(g, eh)] = keep.tile([P, 512, 4], BF16, name="wgrp%d%d" % (g, eh), align_bytes=64)
-                copy_on(
-                    s,
-                    wgrp[(g, eh)][:].rearrange("p (c i) t -> p c t i", i=4),
-                    wraw[(g, eh)][:].rearrange("p t (c i) -> p c t i", i=4),
-                )
+                if s in ON_GPSIMD:
+                    for cc in range(4):
+                        nc.gpsimd.tensor_scalar(
+                            out=wgrp[(g, eh)][:, P * cc:P * (cc + 1), :],
+                            in0=wraw[(g, eh)][:, :, P * cc:P * (cc + 1)].rearrange("p t n -> p n t"),
+                            scalar1=1.0, scalar2=0.0, op0=ALU.mult, op1=ALU.add,
+                        )
+                else:
+                    copy_on(
+                        s,
+                        wgrp[(g, eh)][:].rearrange("p (c i) t -> p c t i", i=4),
+                        wraw[(g, eh)][:].rearrange("p t (c i) -> p c t i", i=4),
+                    )
             elif s.startswith("Qw"):
                 g = int(s[2])
                 eh = int(s[3])

@@ -15,61 +15,60 @@ ACT = mybir.ActivationFunctionType
 FLOPS = 2 * 1024 * 1024 * 1024
 
 P = 128
-VW = [1280,1280]
-LOADS = ["z00","z01","z10","z11","W00","W10","x00","x10","W01","W11","x01","x11"]
-ON_VECTOR = ["E1_02","E2_00","E2_01","E1_10","E2_11","E2_12","E3_101"]
-ON_GPSIMD = ["Iw00","Iw10","Iw01","Iw11"]
-STEPS = ["wdS00","wdV00","wdV01","wdS01","wdV10","wdS10","T1_00","T1_01","wdV11","B0","E1_00","T1_02","E1_01","T1_03","E1_02","Iw00","B1","T2_00","E1_03","wdS11","T2_010","T2_011","T2_012","E2_00","T2_013","T1_10","E2_03","E2_01","T1_11","E2_02","Iw10","B2","Qw00","T1_12","E1_10","E1_11","T1_13","E1_12","Qz00","T2_10","E1_13","Qz01","T2_110","T2_111","T2_112","Qw10","Iw01","E2_10","T2_113","E2_11","E2_13","MX00","E2_12","MX10","Qz10","MX20","Qz11","MX30","Iw11","ST00","MX01","ST10","MX11","ST30","MX21","ST20","MX31","Qw01","T3_000","Qw11","T3_010","E3_000","T3_020","ST11","T3_030","ST01","MX40","E3_030","ST21","MX50","E3_020","ST31","MX60","MX70","ST60","T3_100","ST40","T3_110","T3_120","ST50","E3_110","T3_130","ST70","MX41","E3_120","MX51","E3_100","ST41","MX61","E3_010","ST51","MX71","E3_130","T3_001","ST71","T3_011","E3_001","T3_021","ST61","T3_031","E3_021","T3_101","T3_111","E3_011","E3_101","T3_121","T3_131","E3_031","E3_111","E3_131","E3_121"]
-MANUAL = True
-WARM_T = 0
-WARM_MM = 0
+BANK = 512
+PSUM_BANKS = 8
+
+ROUNDS = [(0, 0), (1, 0), (0, 1), (1, 1)]
+
+Z_PIECES = [4, 2]
+VECTOR_SHARE = (5, 8)
+
+ROUND1_ON_VECTOR = [(0, 0), (0, 1), (1, 2)]
+ROUND2_ON_VECTOR = [(0, 0)]
+ROWS_ON_VECTOR = [(1, 1, 1), (1, 3, 1)]
+W_GROUP_ON_SCALAR = [(0, 1)]
 
 
 def tile_functatransformer_pb_kernel(tc, z_heads_bytes, z_heads_scale, x, Wo, bo, out):
     nc = tc.nc
     with ExitStack() as ctx:
         keep = ctx.enter_context(tc.tile_pool(name="keep", bufs=1))
-        psum = ctx.enter_context(tc.psum_pool(name="psum", bufs=8))
-        if MANUAL:
-            ctx.enter_context(tc.manual_schedule())
+        psum = ctx.enter_context(tc.psum_pool(name="psum", bufs=PSUM_BANKS))
+        ctx.enter_context(tc.manual_schedule())
 
-        wz = keep.tile([P, 512], BF16, name="wz")
-        nc.vector.memset(wz[:], 0.0)
-        if WARM_MM > 0:
-            wmm = psum.tile([P, 512], F32, name="wmm", tag="bank")
-            for i in range(WARM_MM):
-                nc.tensor.matmul(out=wmm[:], lhsT=wz[:, 0:P], rhs=wz[:], start=True, stop=True)
-        sc = keep.tile([P, 1], F32, name="sc")
+        def copy_out(on_vector, dst, src):
+            if on_vector:
+                nc.vector.tensor_copy(out=dst, in_=src)
+            else:
+                nc.scalar.copy(out=dst, in_=src)
+
+        scale = keep.tile([P, 1], F32, name="scale")
         scale_rows = z_heads_scale.rearrange("a b h c d -> h (a b c d)")
         for sh in range(4):
-            nc.scalar.dma_start(out=sc[sh:P:4, :], in_=scale_rows)
-        bz = keep.tile([P, P], BF16, name="bz")
-        nc.gpsimd.memset(bz[:], 0.0)
-        nc.scalar.dma_start(out=bz[0:8, :], in_=bo.rearrange("(et p) -> et p", p=P))
+            nc.scalar.dma_start(out=scale[sh:P:4, :], in_=scale_rows)
+        bo_rows = keep.tile([P, P], BF16, name="bo_rows")
+        nc.gpsimd.memset(bo_rows[:], 0.0)
+        nc.scalar.dma_start(out=bo_rows[0:8, :], in_=bo.rearrange("(et p) -> et p", p=P))
 
-        zb = {}
-        wraw = {}
-        xs = {}
-        wo_v = Wo.rearrange("(g p t) n -> g p t n", g=2, p=P, t=4)
-        for name in LOADS:
-            i = int(name[1])
-            if name.startswith("z"):
-                h = int(name[2])
-                t = keep.tile([P, 4, 512], U8, name="zbytes%d%d" % (i, h))
-                src = z_heads_bytes[i].rearrange("w h (sh sl) d -> (h sh) w (sl d)", sh=4)
-                nc.sync.dma_start(out=t[:], in_=src[:, 4 * h:4 * h + 4, :])
-                zb[(i, h)] = t
-            elif name.startswith("W"):
-                eh = int(name[2])
-                t = keep.tile([P, 4, 512], BF16, name="wraw%d%d" % (i, eh))
-                nc.sync.dma_start(out=t[:], in_=wo_v[i][:, :, 512 * eh:512 * (eh + 1)])
-                wraw[(i, eh)] = t
-            else:
-                eh = int(name[2])
-                t = keep.tile([P, 4, 512], BF16, name="xs%d%d" % (i, eh))
-                src = x[i].rearrange("(et p) i j -> p et (i j)", p=P)
-                nc.sync.dma_start(out=t[:], in_=src[:, 4 * eh:4 * eh + 4, :])
-                xs[(i, eh)] = t
+        zbytes = {}
+        for b in range(2):
+            z_src = z_heads_bytes[b].rearrange("w h (sh sl) d -> (h sh) w (sl d)", sh=4)
+            windows = 8 // Z_PIECES[b]
+            for piece in range(Z_PIECES[b]):
+                zbytes[(b, piece)] = keep.tile([P, windows, 512], U8, name="zbytes%d%d" % (b, piece))
+                nc.sync.dma_start(out=zbytes[(b, piece)][:], in_=z_src[:, windows * piece:windows * (piece + 1), :])
+        w_raw = {}
+        wo_src = Wo.rearrange("(g p t) n -> g p t n", g=2, p=P, t=4)
+        for eh in range(2):
+            for g in range(2):
+                w_raw[(g, eh)] = keep.tile([P, 4, BANK], BF16, name="w_raw%d%d" % (g, eh))
+                nc.sync.dma_start(out=w_raw[(g, eh)][:], in_=wo_src[g][:, :, BANK * eh:BANK * (eh + 1)])
+        x_sb = {}
+        for b in range(2):
+            x_src = x[b].rearrange("(et p) i j -> p et (i j)", p=P)
+            for eh in range(2):
+                x_sb[(b, eh)] = keep.tile([P, 4, BANK], BF16, name="x_sb%d%d" % (b, eh))
+                nc.sync.dma_start(out=x_sb[(b, eh)][:], in_=x_src[:, 4 * eh:4 * eh + 4, :])
 
         warm = keep.tile([P, 2], F32, name="warm")
         nc.vector.memset(warm[:], 0.0)
@@ -77,179 +76,157 @@ def tile_functatransformer_pb_kernel(tc, z_heads_bytes, z_heads_scale, x, Wo, bo
 
         ident = keep.tile([P, P], F32, name="ident")
         make_identity(nc, ident[:])
-        p1 = keep.tile([P, P], F32, name="p1")
+        perm_heads = keep.tile([P, P], F32, name="perm_heads")
         nc.vector.tensor_copy(
-            out=p1[:].rearrange("p (g s h) -> p g s h", g=2, s=4),
+            out=perm_heads[:].rearrange("p (g s h) -> p g s h", g=2, s=4),
             in_=ident[:].rearrange("p (g h s) -> p g s h", g=2, s=4),
         )
-        pa = keep.tile([P, P], F32, name="pa")
-        pa_v = pa[:].rearrange("p (w s j) -> p w s j", w=4, s=2)
+        perm_low = keep.tile([P, P], F32, name="perm_low")
+        low_v = perm_low[:].rearrange("p (w s j) -> p w s j", w=4, s=2)
         id_v = ident[:].rearrange("p (w v s k) -> p w v s k", w=4, v=2, s=2)
-        nc.vector.tensor_copy(out=pa_v[:, :, :, 4:12], in_=id_v[:, :, 0, :, 0:8])
-        nc.vector.tensor_copy(out=pa_v[:, :, :, 12:16], in_=id_v[:, :, 1, :, 0:4])
-        nc.vector.tensor_copy(out=pa_v[:, :, :, 0:4], in_=id_v[:, :, 1, :, 4:8])
-        pb = keep.tile([P, P], F32, name="pb")
-        nc.vector.tensor_copy(out=pb[:, 32:128], in_=pa[:, 0:96])
-        nc.vector.tensor_copy(out=pb[:, 0:32], in_=pa[:, 96:128])
-        bzf = keep.tile([P, P], F32, name="bzf")
-        bo_col = keep.tile([P, 8], F32, name="bo_col")
+        nc.vector.tensor_copy(out=low_v[:, :, :, 4:12], in_=id_v[:, :, 0, :, 0:8])
+        nc.vector.tensor_copy(out=low_v[:, :, :, 12:16], in_=id_v[:, :, 1, :, 0:4])
+        nc.vector.tensor_copy(out=low_v[:, :, :, 0:4], in_=id_v[:, :, 1, :, 4:8])
+        perm_high = keep.tile([P, P], F32, name="perm_high")
+        nc.vector.tensor_copy(out=perm_high[:, 32:128], in_=perm_low[:, 0:96])
+        nc.vector.tensor_copy(out=perm_high[:, 0:32], in_=perm_low[:, 96:128])
 
-        if WARM_T > 0:
-            wps = psum.tile([P, 4, P], F32, name="wps", tag="bank")
-            for i in range(WARM_T):
-                nc.tensor.transpose(out=wps[:, i % 4, :], in_=ident[:], identity=ident[:])
-
-        a = {}
-        c = {}
-        gq = {}
+        z_bf = {}
+        z_tok = {}
+        z_k = {}
         for b in range(2):
-            a[b] = keep.tile([P, 4096], BF16, name="a%d" % b)
-            c[b] = keep.tile([P, 2, P, 8], F32, name="c%d" % b)
-            gq[b] = keep.tile([P, 4096], BF16, name="gq%d" % b, align_bytes=64)
-        bank = {}
-        zc = {}
-        zs = {}
-        wgrp = {}
-        wc = {}
-        ws = {}
-        res = {}
-        out_v = out.rearrange("b i j e -> b (i j) e")
+            z_bf[b] = keep.tile([P, 4096], BF16, name="z_bf%d" % b)
+            z_tok[b] = keep.tile([P, 2, P, 8], F32, name="z_tok%d" % b)
+            z_k[b] = keep.tile([P, 4096], BF16, name="z_k%d" % b, align_bytes=64)
+        z_codes = {}
+        z_scales = {}
+        w_grouped = {}
+        w_codes = {}
+        w_scales = {}
+        sums = {}
+        out_rows = out.rearrange("b i j e -> b (i j) e")
 
-        def copy_on(name, o, i):
-            if name in ON_VECTOR:
-                nc.vector.tensor_copy(out=o, in_=i)
-            else:
-                nc.scalar.copy(out=o, in_=i)
+        def widen(b):
+            cols = 4096 // Z_PIECES[b]
+            v_cols = cols * VECTOR_SHARE[0] // VECTOR_SHARE[1]
+            for piece in range(Z_PIECES[b]):
+                src = zbytes[(b, piece)][:].rearrange("p w c -> p (w c)").bitcast(FP8)
+                dst = z_bf[b][:, cols * piece:cols * (piece + 1)]
+                nc.vector.tensor_scalar(
+                    out=dst[:, 0:v_cols], in0=src[:, 0:v_cols], scalar1=scale[:, 0:1], scalar2=None, op0=ALU.mult
+                )
+                nc.scalar.activation(out=dst[:, v_cols:cols], in_=src[:, v_cols:cols], func=ACT.Copy, scale=scale[:, 0:1])
 
-        for s in STEPS:
-            if s.startswith("wd"):
-                b = int(s[3])
-                h = int(s[4])
-                zf = zb[(b, h)][:].rearrange("p w c -> p (w c)").bitcast(FP8)
-                dst = a[b][:, 2048 * h:2048 * (h + 1)]
-                v = VW[b]
-                if s[2] == "V":
-                    nc.vector.tensor_scalar(out=dst[:, 0:v], in0=zf[:, 0:v], scalar1=sc[:, 0:1], scalar2=None, op0=ALU.mult)
-                else:
-                    nc.scalar.activation(out=dst[:, v:2048], in_=zf[:, v:2048], func=ACT.Copy, scale=sc[:, 0:1])
-            elif s.startswith("T1_"):
-                b = int(s[3])
-                k = int(s[4])
-                t1 = psum.tile([P, 4, P], F32, name="t1", tag="bank")
-                aw = a[b][:].bitcast(F32)
-                for j in range(4):
-                    dp = 2 * (4 * (k % 2) + j) + k // 2
-                    nc.tensor.transpose(out=t1[:, j, :], in_=aw[:, dp:2048:16], identity=p1[:])
-                bank[s] = t1
-            elif s.startswith("E1_"):
-                b = int(s[3])
-                k = int(s[4])
+        def tokens_to_partitions(b):
+            words = z_bf[b][:].bitcast(F32)
+            for k in range(4):
+                u = k // 2
                 dq0 = 4 * (k % 2)
-                copy_on(s, c[b][:, k // 2, :, dq0:dq0 + 4], bank["T1_" + s[3:]][:].rearrange("p s x -> p x s"))
-            elif s.startswith("T2_"):
-                b = int(s[3])
-                u = int(s[4])
-                cw = c[b][:].rearrange("p u x q -> p u (x q)")
-                if u == 0:
-                    shs = [0, 1, 2, 3]
-                    for sh in shs:
-                        t2 = psum.tile([P, 2, 2, P], F32, name="t2", tag="bank")
-                        bank["T2_%d%d" % (b, sh)] = t2
-                else:
-                    shs = [int(s[5])]
-                for sh in shs:
-                    perm = pa if sh < 2 else pb
+                bank = psum.tile([P, 4, P], F32, name="round1", tag="bank")
+                for j in range(4):
+                    dp = 2 * (dq0 + j) + u
+                    nc.tensor.transpose(out=bank[:, j, :], in_=words[:, dp:2048:16], identity=perm_heads[:])
+                copy_out((b, k) in ROUND1_ON_VECTOR, z_tok[b][:, u, :, dq0:dq0 + 4], bank[:].rearrange("p s x -> p x s"))
+
+        def k_to_partitions(b):
+            words = z_tok[b][:].rearrange("p u x q -> p u (x q)")
+            banks = []
+            for sh in range(4):
+                bank = psum.tile([P, 2, 2, P], F32, name="round2", tag="bank")
+                banks.append(bank)
+            for u in range(2):
+                for sh in range(4):
+                    perm = perm_low if sh < 2 else perm_high
                     for g in range(2):
                         y = 4 * g + sh
-                        nc.tensor.transpose(out=bank["T2_%d%d" % (b, sh)][:, u, g, :], in_=cw[:, u, y * P:(y + 1) * P], identity=perm[:])
-            elif s.startswith("E2_"):
-                b = int(s[3])
-                sh = int(s[4])
+                        nc.tensor.transpose(out=banks[sh][:, u, g, :], in_=words[:, u, y * P:(y + 1) * P], identity=perm[:])
+            k_words = z_k[b][:].bitcast(F32).rearrange("p (y r) -> p y r", y=8)
+            for sh in range(4):
                 r0 = 32 * ((2 * sh + 4) % 8)
-                gw = gq[b][:].bitcast(F32).rearrange("p (y r) -> p y r", y=8)
-                copy_on(
-                    s,
-                    gw[:, :, r0:r0 + 64].rearrange("p y (x u) -> p y x u", u=2),
-                    bank["T2_%d%d" % (b, sh)][:].rearrange("p u g (w x) -> p (g w) x u", w=4),
+                copy_out(
+                    (b, sh) in ROUND2_ON_VECTOR,
+                    k_words[:, :, r0:r0 + 64].rearrange("p y (x u) -> p y x u", u=2),
+                    banks[sh][:].rearrange("p u g (w x) -> p (g w) x u", w=4),
                 )
-            elif s.startswith("Qz"):
-                b = int(s[2])
-                g = int(s[3])
-                zc[(b, g)] = keep.tile([P, 512], U32, name="zc%d%d" % (b, g), align_bytes=64)
-                zs[(b, g)] = keep.tile([P, 512], U8, name="zs%d%d" % (b, g), align_bytes=64)
-                nc.vector.quantize_mx(out=zc[(b, g)][:].bitcast(FP8X4), scales=zs[(b, g)][:], in_=gq[b][:, 2048 * g:2048 * (g + 1)])
-            elif s.startswith("Iw"):
-                g = int(s[2])
-                eh = int(s[3])
-                wgrp[(g, eh)] = keep.tile([P, 512, 4], BF16, name="wgrp%d%d" % (g, eh), align_bytes=64)
-                if s in ON_GPSIMD:
-                    for cc in range(4):
-                        nc.gpsimd.tensor_scalar(
-                            out=wgrp[(g, eh)][:, P * cc:P * (cc + 1), :],
-                            in0=wraw[(g, eh)][:, :, P * cc:P * (cc + 1)].rearrange("p t n -> p n t"),
-                            scalar1=1.0, scalar2=0.0, op0=ALU.mult, op1=ALU.add,
-                        )
-                else:
-                    copy_on(
-                        s,
-                        wgrp[(g, eh)][:].rearrange("p (c i) t -> p c t i", i=4),
-                        wraw[(g, eh)][:].rearrange("p t (c i) -> p c t i", i=4),
-                    )
-            elif s.startswith("Qw"):
-                g = int(s[2])
-                eh = int(s[3])
-                wc[(g, eh)] = keep.tile([P, 512], U32, name="wc%d%d" % (g, eh), align_bytes=64)
-                ws[(g, eh)] = keep.tile([P, 512], U8, name="ws%d%d" % (g, eh), align_bytes=64)
-                nc.vector.quantize_mx(out=wc[(g, eh)][:].bitcast(FP8X4), scales=ws[(g, eh)][:], in_=wgrp[(g, eh)][:].rearrange("p n t -> p (n t)"))
-            elif s.startswith("MX"):
-                et = int(s[2])
-                b = int(s[3])
-                eh = et // 4
-                el = et % 4
-                acc = psum.tile([P, 512], F32, name="acc", tag="bank")
+
+        def quantize_z(b):
+            for g in range(2):
+                z_codes[(b, g)] = keep.tile([P, BANK], U32, name="z_codes%d%d" % (b, g), align_bytes=64)
+                z_scales[(b, g)] = keep.tile([P, BANK], U8, name="z_scales%d%d" % (b, g), align_bytes=64)
+                nc.vector.quantize_mx(
+                    out=z_codes[(b, g)][:].bitcast(FP8X4), scales=z_scales[(b, g)][:], in_=z_k[b][:, 2048 * g:2048 * (g + 1)]
+                )
+
+        def group_w(g, eh):
+            w_grouped[(g, eh)] = keep.tile([P, BANK, 4], BF16, name="w_grouped%d%d" % (g, eh), align_bytes=64)
+            copy_out(
+                (g, eh) not in W_GROUP_ON_SCALAR,
+                w_grouped[(g, eh)][:].rearrange("p (c i) t -> p c t i", i=4),
+                w_raw[(g, eh)][:].rearrange("p t (c i) -> p c t i", i=4),
+            )
+
+        def quantize_w(g, eh):
+            w_codes[(g, eh)] = keep.tile([P, BANK], U32, name="w_codes%d%d" % (g, eh), align_bytes=64)
+            w_scales[(g, eh)] = keep.tile([P, BANK], U8, name="w_scales%d%d" % (g, eh), align_bytes=64)
+            nc.vector.quantize_mx(
+                out=w_codes[(g, eh)][:].bitcast(FP8X4),
+                scales=w_scales[(g, eh)][:],
+                in_=w_grouped[(g, eh)][:].rearrange("p n t -> p (n t)"),
+            )
+
+        def project(eh, b):
+            for el in range(4):
+                et = 4 * eh + el
+                acc = psum.tile([P, BANK], F32, name="acc", tag="bank")
                 for g in range(2):
                     nc.tensor.matmul_mx(
                         out=acc[:],
-                        lhsT=wc[(g, eh)][:, P * el:P * (el + 1)].bitcast(FP8X4),
-                        lhsT_scale=ws[(g, eh)][:, P * el:P * (el + 1)],
-                        rhs=zc[(b, g)][:].bitcast(FP8X4),
-                        rhs_scale=zs[(b, g)][:],
+                        lhsT=w_codes[(g, eh)][:, P * el:P * (el + 1)].bitcast(FP8X4),
+                        lhsT_scale=w_scales[(g, eh)][:, P * el:P * (el + 1)],
+                        rhs=z_codes[(b, g)][:].bitcast(FP8X4),
+                        rhs_scale=z_scales[(b, g)][:],
                         start=(g == 0),
                         stop=(g == 1),
                     )
-                bank[s] = acc
-            elif s.startswith("ST"):
-                et = int(s[2])
-                b = int(s[3])
-                res[(et, b)] = keep.tile([P, 512], F32, name="res%d%d" % (et, b))
+                sums[(et, b)] = keep.tile([P, BANK], F32, name="sums%d%d" % (et, b))
                 nc.vector.scalar_tensor_tensor(
-                    out=res[(et, b)][:], in0=bank["MX" + s[2:]][:], scalar=bo_col[:, et:et + 1],
-                    in1=xs[(b, et // 4)][:, et % 4, :], op0=ALU.add, op1=ALU.add,
+                    out=sums[(et, b)][:], in0=acc[:], scalar=bo_col[:, et:et + 1],
+                    in1=x_sb[(b, eh)][:, el, :], op0=ALU.add, op1=ALU.add,
                 )
-            elif s.startswith("T3_"):
-                b = int(s[3])
-                pt = int(s[4])
-                eh = int(s[5])
-                t3 = psum.tile([P, 4, P], F32, name="t3", tag="bank")
+
+        def store(eh, b):
+            for pt in range(4):
+                bank = psum.tile([P, 4, P], F32, name="turned", tag="bank")
                 for el in range(4):
-                    nc.tensor.transpose(out=t3[:, el, :], in_=res[(4 * eh + el, b)][:, P * pt:P * (pt + 1)], identity=ident[:])
-                bank[s] = t3
-            elif s.startswith("E3_"):
-                b = int(s[3])
-                pt = int(s[4])
-                eh = int(s[5])
-                o = keep.tile([P, 512], F32, name="o" + s[3:])
-                copy_on(s, o[:], bank["T3_" + s[3:]][:].rearrange("p s x -> p (s x)"))
-                nc.sync.dma_start(out=out_v[b, P * pt:P * (pt + 1), 512 * eh:512 * (eh + 1)], in_=o[:])
-            elif s == "D":
-                nc.tensor.matmul(out=wmm[:], lhsT=wz[:, 0:P], rhs=wz[:], start=True, stop=True)
-            elif s == "B0":
-                nc.vector.tensor_copy(out=bzf[:], in_=bz[:])
-            elif s == "B1":
-                bo_ps = psum.tile([P, 512], F32, name="bo_ps", tag="bank")
-                nc.tensor.transpose(out=bo_ps[:, 0:P], in_=bzf[:], identity=ident[:])
-                bank[s] = bo_ps
-            elif s == "B2":
-                nc.vector.tensor_copy(out=bo_col[:], in_=bank["B1"][:, 0:8])
-            else:
-                assert False, s
+                    nc.tensor.transpose(out=bank[:, el, :], in_=sums[(4 * eh + el, b)][:, P * pt:P * (pt + 1)], identity=ident[:])
+                rows = keep.tile([P, BANK], F32, name="rows%d%d%d" % (b, pt, eh))
+                copy_out((b, pt, eh) in ROWS_ON_VECTOR, rows[:], bank[:].rearrange("p s x -> p (s x)"))
+                nc.sync.dma_start(out=out_rows[b, P * pt:P * (pt + 1), BANK * eh:BANK * (eh + 1)], in_=rows[:])
+
+        widen(0)
+        widen(1)
+        bo_f32 = keep.tile([P, P], F32, name="bo_f32")
+        nc.vector.tensor_copy(out=bo_f32[:], in_=bo_rows[:])
+        tokens_to_partitions(0)
+        group_w(0, 0)
+        group_w(1, 0)
+        bo_bank = psum.tile([P, BANK], F32, name="bo_bank", tag="bank")
+        nc.tensor.transpose(out=bo_bank[:, 0:P], in_=bo_f32[:], identity=ident[:])
+        k_to_partitions(0)
+        bo_col = keep.tile([P, 8], F32, name="bo_col")
+        nc.vector.tensor_copy(out=bo_col[:], in_=bo_bank[:, 0:8])
+        quantize_w(0, 0)
+        quantize_w(1, 0)
+        quantize_z(0)
+        tokens_to_partitions(1)
+        group_w(0, 1)
+        group_w(1, 1)
+        k_to_partitions(1)
+        quantize_w(0, 1)
+        quantize_w(1, 1)
+        project(*ROUNDS[0])
+        quantize_z(1)
+        for r in range(1, 4):
+            project(*ROUNDS[r])
+            store(*ROUNDS[r - 1])
+        store(*ROUNDS[3])

@@ -21,7 +21,7 @@ PSUM_BANKS = 8
 ROUNDS = [(0, 0), (1, 0), (0, 1), (1, 1)]
 
 Z_PIECES = [4, 2]
-VECTOR_SHARE = (5, 8)
+VECTOR_SHARE = [(3, 4), (5, 8)]
 
 ROUND1_ON_VECTOR = [(0, 0), (0, 1), (1, 2)]
 ROUND2_ON_VECTOR = [(0, 0)]
@@ -42,13 +42,8 @@ def tile_functatransformer_pb_kernel(tc, z_heads_bytes, z_heads_scale, x, Wo, bo
             else:
                 nc.scalar.copy(out=dst, in_=src)
 
-        scale = keep.tile([P, 1], F32, name="scale")
-        scale_rows = z_heads_scale.rearrange("a b h c d -> h (a b c d)")
-        for sh in range(4):
-            nc.scalar.dma_start(out=scale[sh:P:4, :], in_=scale_rows)
-        bo_rows = keep.tile([P, P], BF16, name="bo_rows")
-        nc.gpsimd.memset(bo_rows[:], 0.0)
-        nc.scalar.dma_start(out=bo_rows[0:8, :], in_=bo.rearrange("(et p) -> et p", p=P))
+        all_scales = keep.tile([P, 32], F32, name="all_scales")
+        nc.scalar.dma_start(out=all_scales[:], in_=z_heads_scale.rearrange("a b h c d -> (a b h c d)").partition_broadcast(P))
 
         zbytes = {}
         for b in range(2):
@@ -69,6 +64,9 @@ def tile_functatransformer_pb_kernel(tc, z_heads_bytes, z_heads_scale, x, Wo, bo
             for eh in range(2):
                 x_sb[(b, eh)] = keep.tile([P, 4, BANK], BF16, name="x_sb%d%d" % (b, eh))
                 nc.sync.dma_start(out=x_sb[(b, eh)][:], in_=x_src[:, 4 * eh:4 * eh + 4, :])
+        bo_col = keep.tile([P, 8, 2], BF16, name="bo_col")
+        with nc.allow_non_contiguous_dma(reason="1,024 single values of the bias, one to a partition and channel tile"):
+            nc.sync.dma_start(out=bo_col[:, :, 0:1], in_=bo.rearrange("(et p one) -> p et one", p=P, one=1))
 
         warm = keep.tile([P, 2], F32, name="warm")
         nc.vector.memset(warm[:], 0.0)
@@ -76,6 +74,10 @@ def tile_functatransformer_pb_kernel(tc, z_heads_bytes, z_heads_scale, x, Wo, bo
 
         ident = keep.tile([P, P], F32, name="ident")
         make_identity(nc, ident[:])
+        own_head = keep.tile([P, 32], F32, name="own_head")
+        nc.vector.tensor_reduce(
+            out=own_head[:], in_=ident[:].rearrange("p (h s) -> p h s", s=4), op=ALU.add, axis=mybir.AxisListType.X
+        )
         perm_heads = keep.tile([P, P], F32, name="perm_heads")
         nc.vector.tensor_copy(
             out=perm_heads[:].rearrange("p (g s h) -> p g s h", g=2, s=4),
@@ -90,6 +92,11 @@ def tile_functatransformer_pb_kernel(tc, z_heads_bytes, z_heads_scale, x, Wo, bo
         perm_high = keep.tile([P, P], F32, name="perm_high")
         nc.vector.tensor_copy(out=perm_high[:, 32:128], in_=perm_low[:, 0:96])
         nc.vector.tensor_copy(out=perm_high[:, 0:32], in_=perm_low[:, 96:128])
+
+        own_scale = keep.tile([P, 32], F32, name="own_scale")
+        nc.vector.tensor_tensor(out=own_scale[:], in0=all_scales[:], in1=own_head[:], op=ALU.mult)
+        scale = keep.tile([P, 1], F32, name="scale")
+        nc.vector.tensor_reduce(out=scale[:], in_=own_scale[:], op=ALU.add, axis=mybir.AxisListType.X)
 
         z_bf = {}
         z_tok = {}
@@ -108,7 +115,7 @@ def tile_functatransformer_pb_kernel(tc, z_heads_bytes, z_heads_scale, x, Wo, bo
 
         def widen(b):
             cols = 4096 // Z_PIECES[b]
-            v_cols = cols * VECTOR_SHARE[0] // VECTOR_SHARE[1]
+            v_cols = cols * VECTOR_SHARE[b][0] // VECTOR_SHARE[b][1]
             for piece in range(Z_PIECES[b]):
                 src = zbytes[(b, piece)][:].rearrange("p w c -> p (w c)").bitcast(FP8)
                 dst = z_bf[b][:, cols * piece:cols * (piece + 1)]
@@ -190,7 +197,7 @@ def tile_functatransformer_pb_kernel(tc, z_heads_bytes, z_heads_scale, x, Wo, bo
                     )
                 sums[(et, b)] = keep.tile([P, BANK], F32, name="sums%d%d" % (et, b))
                 nc.vector.scalar_tensor_tensor(
-                    out=sums[(et, b)][:], in0=acc[:], scalar=bo_col[:, et:et + 1],
+                    out=sums[(et, b)][:], in0=acc[:], scalar=bo_col[:, et, 0:1],
                     in1=x_sb[(b, eh)][:, el, :], op0=ALU.add, op1=ALU.add,
                 )
 
@@ -205,16 +212,10 @@ def tile_functatransformer_pb_kernel(tc, z_heads_bytes, z_heads_scale, x, Wo, bo
 
         widen(0)
         widen(1)
-        bo_f32 = keep.tile([P, P], F32, name="bo_f32")
-        nc.vector.tensor_copy(out=bo_f32[:], in_=bo_rows[:])
         tokens_to_partitions(0)
         group_w(0, 0)
         group_w(1, 0)
-        bo_bank = psum.tile([P, BANK], F32, name="bo_bank", tag="bank")
-        nc.tensor.transpose(out=bo_bank[:, 0:P], in_=bo_f32[:], identity=ident[:])
         k_to_partitions(0)
-        bo_col = keep.tile([P, 8], F32, name="bo_col")
-        nc.vector.tensor_copy(out=bo_col[:], in_=bo_bank[:, 0:8])
         quantize_w(0, 0)
         quantize_w(1, 0)
         quantize_z(0)

@@ -227,7 +227,10 @@ def tile_functatransformer_pb_kernel(tc, z_heads_bytes, z_heads_scale, x, Wo, bo
         quantize_w(1, 1)
         project(*ROUNDS[0])
         quantize_z(1)
-        for r in range(1, 4):
-            project(*ROUNDS[r])
-            store(*ROUNDS[r - 1])
+        project(*ROUNDS[1])
+        store(*ROUNDS[0])
+        project(*ROUNDS[2])
+        store(*ROUNDS[1])
+        store(*ROUNDS[2])
+        project(*ROUNDS[3])
         store(*ROUNDS[3])

@@ -210,6 +210,23 @@ def tile_functatransformer_pb_kernel(tc, z_heads_bytes, z_heads_scale, x, Wo, bo
                 copy_out((b, pt, eh) in ROWS_ON_VECTOR, rows[:], bank[:].rearrange("p s x -> p (s x)"))
                 nc.sync.dma_start(out=out_rows[b, P * pt:P * (pt + 1), BANK * eh:BANK * (eh + 1)], in_=rows[:])
 
+        def store_by_pairs(eh, b):
+            for pair in range(2):
+                for half in range(2):
+                    bank = psum.tile([P, 2, 2, P], F32, name="turned_pair", tag="bank")
+                    for t in range(2):
+                        pt = 2 * half + t
+                        for e2 in range(2):
+                            nc.tensor.transpose(
+                                out=bank[:, t, e2, :], in_=sums[(4 * eh + 2 * pair + e2, b)][:, P * pt:P * (pt + 1)], identity=ident[:]
+                            )
+                    rows = keep.tile([P, 2, 2 * P], F32, name="pair_rows%d%d" % (pair, half))
+                    copy_out(half == 1, rows[:], bank[:].rearrange("p t s x -> p t (s x)"))
+                    c0 = BANK * eh + 2 * P * pair
+                    nc.sync.dma_start(
+                        out=out_rows[b, 2 * P * half:2 * P * (half + 1), c0:c0 + 2 * P].rearrange("(t p) e -> p t e", p=P), in_=rows[:]
+                    )
+
         widen(0)
         widen(1)
         tokens_to_partitions(0)
@@ -233,4 +250,4 @@ def tile_functatransformer_pb_kernel(tc, z_heads_bytes, z_heads_scale, x, Wo, bo
         store(*ROUNDS[1])
         store(*ROUNDS[2])
         project(*ROUNDS[3])
-        store(*ROUNDS[3])
+        store_by_pairs(*ROUNDS[3])

from contextlib import ExitStack

import concourse.mybir as mybir
from concourse.masks import make_identity

F32 = mybir.dt.float32
BF16 = mybir.dt.bfloat16
U8 = mybir.dt.uint8
U32 = mybir.dt.uint32
FP8 = mybir.dt.float8_e4m3fn
FP8X4 = mybir.dt.float8_e4m3fn_x4
ALU = mybir.AluOpType
ACT = mybir.ActivationFunctionType

FLOPS = 2 * 1024 * 1024 * 1024

P = 128
BANK = 512
PSUM_BANKS = 8

ROUNDS = [(0, 0), (1, 0), (0, 1), (1, 1)]

Z_PIECES = [4, 2]
VECTOR_SHARE = [(3, 4), (5, 8)]

ROUND1_ON_VECTOR = [(0, 0), (0, 1), (1, 2)]
ROUND2_ON_VECTOR = [(0, 0)]
ROWS_ON_VECTOR = [(1, 1, 1), (1, 3, 1)]
W_GROUP_ON_SCALAR = [(0, 1)]


def tile_functatransformer_pb_kernel(tc, z_heads_bytes, z_heads_scale, x, Wo, bo, out):
    nc = tc.nc
    with ExitStack() as ctx:
        keep = ctx.enter_context(tc.tile_pool(name="keep", bufs=1))
        psum = ctx.enter_context(tc.psum_pool(name="psum", bufs=PSUM_BANKS))
        ctx.enter_context(tc.manual_schedule())

        def copy_out(on_vector, dst, src):
            if on_vector:
                nc.vector.tensor_copy(out=dst, in_=src)
            else:
                nc.scalar.copy(out=dst, in_=src)

        all_scales = keep.tile([P, 32], F32, name="all_scales")
        nc.scalar.dma_start(out=all_scales[:], in_=z_heads_scale.rearrange("a b h c d -> (a b h c d)").partition_broadcast(P))

        zbytes = {}
        for b in range(2):
            z_src = z_heads_bytes[b].rearrange("w h (sh sl) d -> (h sh) w (sl d)", sh=4)
            windows = 8 // Z_PIECES[b]
            for piece in range(Z_PIECES[b]):
                zbytes[(b, piece)] = keep.tile([P, windows, 512], U8, name="zbytes%d%d" % (b, piece))
                nc.sync.dma_start(out=zbytes[(b, piece)][:], in_=z_src[:, windows * piece:windows * (piece + 1), :])
        w_raw = {}
        wo_src = Wo.rearrange("(g p t) n -> g p t n", g=2, p=P, t=4)
        for eh in range(2):
            for g in range(2):
                w_raw[(g, eh)] = keep.tile([P, 4, BANK], BF16, name="w_raw%d%d" % (g, eh))
                nc.sync.dma_start(out=w_raw[(g, eh)][:], in_=wo_src[g][:, :, BANK * eh:BANK * (eh + 1)])
        x_sb = {}
        for b in range(2):
            x_src = x[b].rearrange("(et p) i j -> p et (i j)", p=P)
            for eh in range(2):
                x_sb[(b, eh)] = keep.tile([P, 4, BANK], BF16, name="x_sb%d%d" % (b, eh))
                nc.sync.dma_start(out=x_sb[(b, eh)][:], in_=x_src[:, 4 * eh:4 * eh + 4, :])
        bo_col = keep.tile([P, 8, 2], BF16, name="bo_col")
        with nc.allow_non_contiguous_dma(reason="1,024 single values of the bias, one to a partition and channel tile"):
            nc.sync.dma_start(out=bo_col[:, :, 0:1], in_=bo.rearrange("(et p one) -> p et one", p=P, one=1))

        warm = keep.tile([P, 2], F32, name="warm")
        nc.vector.memset(warm[:], 0.0)
        nc.scalar.activation(out=warm[:, 1:2], in_=warm[:, 0:1], func=ACT.Copy)

        ident = keep.tile([P, P], F32, name="ident")
        make_identity(nc, ident[:])
        own_head = keep.tile([P, 32], F32, name="own_head")
        nc.vector.tensor_reduce(
            out=own_head[:], in_=ident[:].rearrange("p (h s) -> p h s", s=4), op=ALU.add, axis=mybir.AxisListType.X
        )
        perm_heads = keep.tile([P, P], F32, name="perm_heads")
        nc.vector.tensor_copy(
            out=perm_heads[:].rearrange("p (g s h) -> p g s h", g=2, s=4),
            in_=ident[:].rearrange("p (g h s) -> p g s h", g=2, s=4),
        )
        perm_low = keep.tile([P, P], F32, name="perm_low")
        low_v = perm_low[:].rearrange("p (w s j) -> p w s j", w=4, s=2)
        id_v = ident[:].rearrange("p (w v s k) -> p w v s k", w=4, v=2, s=2)
        nc.vector.tensor_copy(out=low_v[:, :, :, 4:12], in_=id_v[:, :, 0, :, 0:8])
        nc.vector.tensor_copy(out=low_v[:, :, :, 12:16], in_=id_v[:, :, 1, :, 0:4])
        nc.vector.tensor_copy(out=low_v[:, :, :, 0:4], in_=id_v[:, :, 1, :, 4:8])
        perm_high = keep.tile([P, P], F32, name="perm_high")
        nc.vector.tensor_copy(out=perm_high[:, 32:128], in_=perm_low[:, 0:96])
        nc.vector.tensor_copy(out=perm_high[:, 0:32], in_=perm_low[:, 96:128])

        own_scale = keep.tile([P, 32], F32, name="own_scale")
        nc.vector.tensor_tensor(out=own_scale[:], in0=all_scales[:], in1=own_head[:], op=ALU.mult)
        scale = keep.tile([P, 1], F32, name="scale")
        nc.vector.tensor_reduce(out=scale[:], in_=own_scale[:], op=ALU.add, axis=mybir.AxisListType.X)

        z_bf = {}
        z_tok = {}
        z_k = {}
        for b in range(2):
            z_bf[b] = keep.tile([P, 4096], BF16, name="z_bf%d" % b)
            z_tok[b] = keep.tile([P, 2, P, 8], F32, name="z_tok%d" % b)
            z_k[b] = keep.tile([P, 4096], BF16, name="z_k%d" % b, align_bytes=64)
        z_codes = {}
        z_scales = {}
        w_grouped = {}
        w_codes = {}
        w_scales = {}
        sums = {}
        out_rows = out.rearrange("b i j e -> b (i j) e")

        def widen(b):
            cols = 4096 // Z_PIECES[b]
            v_cols = cols * VECTOR_SHARE[b][0] // VECTOR_SHARE[b][1]
            for piece in range(Z_PIECES[b]):
                src = zbytes[(b, piece)][:].rearrange("p w c -> p (w c)").bitcast(FP8)
                dst = z_bf[b][:, cols * piece:cols * (piece + 1)]
                nc.vector.tensor_scalar(
                    out=dst[:, 0:v_cols], in0=src[:, 0:v_cols], scalar1=scale[:, 0:1], scalar2=None, op0=ALU.mult
                )
                nc.scalar.activation(out=dst[:, v_cols:cols], in_=src[:, v_cols:cols], func=ACT.Copy, scale=scale[:, 0:1])

        def tokens_to_partitions(b):
            words = z_bf[b][:].bitcast(F32)
            for k in range(4):
                u = k // 2
                dq0 = 4 * (k % 2)
                bank = psum.tile([P, 4, P], F32, name="round1", tag="bank")
                for j in range(4):
                    dp = 2 * (dq0 + j) + u
                    nc.tensor.transpose(out=bank[:, j, :], in_=words[:, dp:2048:16], identity=perm_heads[:])
                copy_out((b, k) in ROUND1_ON_VECTOR, z_tok[b][:, u, :, dq0:dq0 + 4], bank[:].rearrange("p s x -> p x s"))

        def k_to_partitions(b):
            words = z_tok[b][:].rearrange("p u x q -> p u (x q)")
            banks = []
            for sh in range(4):
                bank = psum.tile([P, 2, 2, P], F32, name="round2", tag="bank")
                banks.append(bank)
            for u in range(2):
                for sh in range(4):
                    perm = perm_low if sh < 2 else perm_high
                    for g in range(2):
                        y = 4 * g + sh
                        nc.tensor.transpose(out=banks[sh][:, u, g, :], in_=words[:, u, y * P:(y + 1) * P], identity=perm[:])
            k_words = z_k[b][:].bitcast(F32).rearrange("p (y r) -> p y r", y=8)
            for sh in range(4):
                r0 = 32 * ((2 * sh + 4) % 8)
                copy_out(
                    (b, sh) in ROUND2_ON_VECTOR,
                    k_words[:, :, r0:r0 + 64].rearrange("p y (x u) -> p y x u", u=2),
                    banks[sh][:].rearrange("p u g (w x) -> p (g w) x u", w=4),
                )

        def quantize_z(b):
            for g in range(2):
                z_codes[(b, g)] = keep.tile([P, BANK], U32, name="z_codes%d%d" % (b, g), align_bytes=64)
                z_scales[(b, g)] = keep.tile([P, BANK], U8, name="z_scales%d%d" % (b, g), align_bytes=64)
                nc.vector.quantize_mx(
                    out=z_codes[(b, g)][:].bitcast(FP8X4), scales=z_scales[(b, g)][:], in_=z_k[b][:, 2048 * g:2048 * (g + 1)]
                )

        def group_w(g, eh):
            w_grouped[(g, eh)] = keep.tile([P, BANK, 4], BF16, name="w_grouped%d%d" % (g, eh), align_bytes=64)
            copy_out(
                (g, eh) not in W_GROUP_ON_SCALAR,
                w_grouped[(g, eh)][:].rearrange("p (c i) t -> p c t i", i=4),
                w_raw[(g, eh)][:].rearrange("p t (c i) -> p c t i", i=4),
            )

        def quantize_w(g, eh):
            w_codes[(g, eh)] = keep.tile([P, BANK], U32, name="w_codes%d%d" % (g, eh), align_bytes=64)
            w_scales[(g, eh)] = keep.tile([P, BANK], U8, name="w_scales%d%d" % (g, eh), align_bytes=64)
            nc.vector.quantize_mx(
                out=w_codes[(g, eh)][:].bitcast(FP8X4),
                scales=w_scales[(g, eh)][:],
                in_=w_grouped[(g, eh)][:].rearrange("p n t -> p (n t)"),
            )

        def project(eh, b):
            for el in range(4):
                et = 4 * eh + el
                acc = psum.tile([P, BANK], F32, name="acc", tag="bank")
                for g in range(2):
                    nc.tensor.matmul_mx(
                        out=acc[:],
                        lhsT=w_codes[(g, eh)][:, P * el:P * (el + 1)].bitcast(FP8X4),
                        lhsT_scale=w_scales[(g, eh)][:, P * el:P * (el + 1)],
                        rhs=z_codes[(b, g)][:].bitcast(FP8X4),
                        rhs_scale=z_scales[(b, g)][:],
                        start=(g == 0),
                        stop=(g == 1),
                    )
                sums[(et, b)] = keep.tile([P, BANK], F32, name="sums%d%d" % (et, b))
                nc.vector.scalar_tensor_tensor(
                    out=sums[(et, b)][:], in0=acc[:], scalar=bo_col[:, et, 0:1],
                    in1=x_sb[(b, eh)][:, el, :], op0=ALU.add, op1=ALU.add,
                )

        def store(eh, b):
            for pt in range(4):
                bank = psum.tile([P, 4, P], F32, name="turned", tag="bank")
                for el in range(4):
                    nc.tensor.transpose(out=bank[:, el, :], in_=sums[(4 * eh + el, b)][:, P * pt:P * (pt + 1)], identity=ident[:])
                rows = keep.tile([P, BANK], F32, name="rows%d%d%d" % (b, pt, eh))
                copy_out((b, pt, eh) in ROWS_ON_VECTOR, rows[:], bank[:].rearrange("p s x -> p (s x)"))
                nc.sync.dma_start(out=out_rows[b, P * pt:P * (pt + 1), BANK * eh:BANK * (eh + 1)], in_=rows[:])

        def store_by_pairs(eh, b):
            for pair in range(2):
                for half in range(2):
                    bank = psum.tile([P, 2, 2, P], F32, name="turned_pair", tag="bank")
                    for t in range(2):
                        pt = 2 * half + t
                        for e2 in range(2):
                            nc.tensor.transpose(
                                out=bank[:, t, e2, :], in_=sums[(4 * eh + 2 * pair + e2, b)][:, P * pt:P * (pt + 1)], identity=ident[:]
                            )
                    rows = keep.tile([P, 2, 2 * P], F32, name="pair_rows%d%d" % (pair, half))
                    copy_out(half == 1, rows[:], bank[:].rearrange("p t s x -> p t (s x)"))
                    c0 = BANK * eh + 2 * P * pair
                    nc.sync.dma_start(
                        out=out_rows[b, 2 * P * half:2 * P * (half + 1), c0:c0 + 2 * P].rearrange("(t p) e -> p t e", p=P), in_=rows[:]
                    )

        widen(0)
        widen(1)
        tokens_to_partitions(0)
        group_w(0, 0)
        group_w(1, 0)
        k_to_partitions(0)
        quantize_w(0, 0)
        quantize_w(1, 0)
        quantize_z(0)
        tokens_to_partitions(1)
        group_w(0, 1)
        group_w(1, 1)
        k_to_partitions(1)
        quantize_w(0, 1)
        quantize_w(1, 1)
        project(*ROUNDS[0])
        quantize_z(1)
        project(*ROUNDS[1])
        store(*ROUNDS[0])
        project(*ROUNDS[2])
        store(*ROUNDS[1])
        store(*ROUNDS[2])
        project(*ROUNDS[3])
        store_by_pairs(*ROUNDS[3])
